import numpy as np
import ml_dtypes


def mxq(x, axis, fmt="e4m3"):
    dtype, down = {"e4m3": (ml_dtypes.float8_e4m3fn, 7), "e5m2": (ml_dtypes.float8_e5m2, 14)}[fmt]
    v = np.moveaxis(np.asarray(x, np.float32).astype(ml_dtypes.bfloat16).astype(np.float64), axis, -1)
    blocks = v.reshape(v.shape[:-1] + (-1, 32))
    amax = np.abs(blocks).max(-1, keepdims=True)
    byte = np.maximum(np.where(amax > 0, np.frexp(amax)[1] - 1 + 127, 0) - down, 1)
    scale = np.exp2(byte - 127.0)
    codes = (blocks / scale).astype(np.float32).astype(dtype).astype(np.float64)
    return np.moveaxis((codes * scale).reshape(v.shape), -1, axis)


WIDE = False


def mx_kscale(k):
    if not WIDE:
        return np.ones(k)
    levels = np.array([10, -10, 5, -5, 0])
    if k % 512:
        return np.exp2(np.random.permutation(np.resize(levels, k // 32))).repeat(32)
    a = np.empty((k // 512, 16))
    for p in range(k // 512):
        a[p, :8] = np.random.permutation(np.resize(levels, 8))
        for g in range(8):
            far = levels[np.abs(levels - a[p, g]) >= 10]
            a[p, g + 8] = far[np.random.randint(len(far))]
    return np.exp2(a.ravel()).repeat(32)


BF16 = ml_dtypes.bfloat16


def bf(x):
    return np.asarray(x, np.float32).astype(BF16)


def f64(x):
    return np.asarray(x).astype(np.float64)


B, HID, UD = 1024, 1024, 512


def sigmoid(v):
    return 1.0 / (1.0 + np.exp(-v))


def setup_inputs():
    s, t, u = mx_kscale(HID), mx_kscale(UD), mx_kscale(UD)
    return {
        "encoder_hidden": bf(np.random.standard_normal((B, HID)) * s),
        "spk_vectors": bf(np.random.standard_normal((B, UD)) * t),
        "adr_vectors": bf(np.random.standard_normal((B, UD)) * u),
        "WA_xp": bf(np.random.standard_normal((UD, HID)) / np.sqrt(HID) / s),
        "WA_hp": bf(np.random.standard_normal((UD, UD)) / np.sqrt(UD) / t),
        "VA_hp": bf(np.random.standard_normal((UD, UD)) / np.sqrt(UD) / u),
        "VA_hh": bf(np.random.standard_normal((UD, UD)) / np.sqrt(UD) / u),
    }


def reference(encoder_hidden, spk_vectors, adr_vectors, WA_xp, WA_hp, VA_hp, VA_hh):
    x, hs, ha = f64(encoder_hidden), f64(spk_vectors), f64(adr_vectors)
    p_t = sigmoid((mxq(x, 1, "e4m3") @ mxq(f64(WA_xp), 1, "e4m3").T)
                  + (mxq(hs, 1, "e4m3") @ mxq(f64(WA_hp), 1, "e4m3").T)
                  + (mxq(ha, 1, "e4m3") @ mxq(f64(VA_hp), 1, "e4m3").T))
    return mxq(p_t * ha, 1, "e4m3") @ mxq(f64(VA_hh), 1, "e4m3").T

@@ -1,0 +1,354 @@
+from contextlib import ExitStack
+
+import concourse.mybir as mybir
+from concourse.masks import make_identity
+
+F32 = mybir.dt.float32
+BF16 = mybir.dt.bfloat16
+U32 = mybir.dt.uint32
+U8 = mybir.dt.uint8
+FP8X4 = mybir.dt.float8_e4m3fn_x4
+SIGMOID = mybir.ActivationFunctionType.Sigmoid
+MULT = mybir.AluOpType.mult
+P = 128
+FLOPS = 2 * 1024 * 512 * (1024 + 512 + 512 + 512)
+
+STEPS = [
+    ("L", "Whp0"),
+    ("L", "Whp1"),
+    ("L", "hs0"),
+    ("L", "Vhp"),
+    ("L", "ha0"),
+    ("L", "x0"),
+    ("L", "Wx0"),
+    ("L", "Wx1"),
+    ("L", "Vhh"),
+    ("L", "hs1"),
+    ("L", "ha1"),
+    ("L", "x1"),
+    ("L", "hs2"),
+    ("L", "ha2"),
+    ("L", "x2"),
+    ("L", "hs3"),
+    ("L", "ha3"),
+    ("L", "x3"),
+    ("T", "Whp0", 4),
+    ("T", "Whp1", 5),
+    ("C", "Whp0", "S"),
+    ("T", "hs0", 6),
+    ("C", "Whp1", "S"),
+    ("Q", "Whp0"),
+    ("C", "hs0", "V"),
+    ("Q", "Whp1"),
+    ("T", "Vhp0", 7),
+    ("Q", "hs0"),
+    ("T", "Vhp1", 4),
+    ("C", "Vhp0", "V"),
+    ("T", "ha0", 5),
+    ("C", "Vhp1", "S"),
+    ("MA", 0),
+    ("Q", "Vhp0"),
+    ("C", "ha0", "S"),
+    ("Q", "Vhp1"),
+    ("T", "x0k0", 6),
+    ("Q", "ha0"),
+    ("T", "x0k1", 7),
+    ("C", "x0k0", "V"),
+    ("MA", 1),
+    ("C", "x0k1", "V"),
+    ("T", "Wx0k0", 4),
+    ("Q", "x0k0"),
+    ("Q", "x0k1"),
+    ("T", "Wx0k1", 5),
+    ("C", "Wx0k0", "V"),
+    ("T", "Wx1k0", 6),
+    ("C", "Wx0k1", "S"),
+    ("T", "Wx1k1", 7),
+    ("Q", "Wx0k0"),
+    ("C", "Wx1k0", "V"),
+    ("T", "Vhh0", 4),
+    ("T", "Vhh1", 5),
+    ("Q", "Wx0k1"),
+    ("T", "hs1", 6),
+    ("Q", "Wx1k0"),
+    ("C", "Vhh1", "S"),
+    ("C", "Wx1k1", "V"),
+    ("MA", 2),
+    ("C", "Vhh0", "V"),
+    ("T", "ha1", 7),
+    ("SA", 0),
+    ("Q", "Wx1k1"),
+    ("SA", 1),
+    ("T", "x1k0", 4),
+    ("Q", "Vhh0"),
+    ("Q", "Vhh1"),
+    ("T", "x1k1", 5),
+    ("C", "hs1", "V"),
+    ("C", "x1k0", "S"),
+    ("MA", 3),
+    ("C", "ha1", "V"),
+    ("C", "x1k1", "S"),
+    ("T", "hs2", 6),
+    ("Q", "hs1"),
+    ("SA", 2),
+    ("T", "ha2", 7),
+    ("Q", "ha1"),
+    ("C", "hs2", "S"),
+    ("Q", "x1k0"),
+    ("T", "x2k0", 4),
+    ("Q", "x1k1"),
+    ("SA", 3),
+    ("T", "x2k1", 5),
+    ("Q", "hs2"),
+    ("C", "x2k0", "S"),
+    ("T", "hs3", 6),
+    ("C", "ha2", "V"),
+    ("MB", 1, 0),
+    ("C", "hs3", "S"),
+    ("Q", "x2k0"),
+    ("Q", "ha2"),
+    ("C", "x2k1", "V"),
+    ("MB", 1, 1),
+    ("SB", 1, 0),
+    ("Q", "hs3"),
+    ("Q", "x2k1"),
+    ("PR", 0, 1),
+    ("T", "ha3", 7),
+    ("SB", 1, 1),
+    ("T", "x3k0", 4),
+    ("QG", 0, 1),
+    ("PR", 1, 1),
+    ("T", "x3k1", 5),
+    ("C", "ha3", "S"),
+    ("S2", 0, 2),
+    ("QG", 1, 1),
+    ("C", "x3k0", "S"),
+    ("MB", 2, 0),
+    ("Q", "ha3"),
+    ("C", "x3k1", "S"),
+    ("Q", "x3k0"),
+    ("OC", 0, "S"),
+    ("S2", 1, 3),
+    ("Q", "x3k1"),
+    ("MB", 2, 1),
+    ("SB", 2, 0),
+    ("OC", 1, "V"),
+    ("PR", 2, 1),
+    ("ST", 0, 2),
+    ("MB", 3, 0),
+    ("SB", 2, 1),
+    ("QG", 2, 1),
+    ("PR", 3, 1),
+    ("S2", 2, 2),
+    ("QG", 3, 1),
+    ("PR", 4, 1),
+    ("MB", 3, 1),
+    ("SB", 3, 0),
+    ("OC", 2, "S"),
+    ("QG", 4, 1),
+    ("PR", 5, 1),
+    ("S2", 3, 3),
+    ("S2", 4, 2),
+    ("SB", 3, 1),
+    ("QG", 5, 1),
+    ("OC", 3, "V"),
+    ("OC", 4, "S"),
+    ("PR", 6, 1),
+    ("ST", 2, 2),
+    ("S2", 5, 3),
+    ("QG", 6, 1),
+    ("OC", 5, "S"),
+    ("PR", 7, 1),
+    ("S2", 6, 2),
+    ("ST", 4, 2),
+    ("QG", 7, 1),
+    ("OC", 6, "S"),
+    ("S2", 7, 3),
+    ("OC", 7, "S"),
+    ("ST", 6, 1),
+    ("ST", 7, 1),
+]
+
+
+def tile_updatespeaker_pa_kernel(
+    tc, encoder_hidden, spk_vectors, adr_vectors, WA_xp, WA_hp, VA_hp, VA_hh, out
+):
+    nc = tc.nc
+    with ExitStack() as ctx:
+        keep = ctx.enter_context(tc.tile_pool(name="keep", bufs=1))
+        psum = ctx.enter_context(tc.psum_pool(name="psum", bufs=1))
+
+        ident = keep.tile([P, P], F32, name="ident")
+        warm_in = keep.tile([P, 1], F32, name="warm_in")
+        warm_out = keep.tile([P, 1], F32, name="warm_out")
+
+        whp_raw = keep.tile([P, 4, 512], BF16, name="whp_raw")
+        vhp_raw = keep.tile([P, 4, 512], BF16, name="vhp_raw")
+        vhh_raw = keep.tile([P, 4, 512], BF16, name="vhh_raw")
+        wxp_raw = keep.tile([P, 4, 1024], BF16, name="wxp_raw")
+        hs_raw = keep.tile([P, 8, 512], BF16, name="hs_raw")
+        ha_raw = keep.tile([P, 8, 512], BF16, name="ha_raw")
+        x_raw = keep.tile([P, 8, 1024], BF16, name="x_raw")
+
+        w_grp = [keep.tile([P, 512, 2], F32, name="w_grp%d" % s, align_bytes=64) for s in range(5)]
+        w_codes = [keep.tile([P, 512], U32, name="w_codes%d" % s, align_bytes=64) for s in range(5)]
+        w_scl = [keep.tile([P, 512], U8, name="w_scl%d" % s, align_bytes=64) for s in range(5)]
+        a_grp = [keep.tile([P, 1024, 2], F32, name="a_grp%d" % s, align_bytes=64) for s in range(4)]
+        a_codes = [keep.tile([P, 1024], U32, name="a_codes%d" % s, align_bytes=64) for s in range(4)]
+        a_scl = [keep.tile([P, 1024], U8, name="a_scl%d" % s, align_bytes=64) for s in range(4)]
+        sig = keep.tile([P, 4, 1024], F32, name="sig")
+        g_grp = keep.tile([P, 1024, 4], BF16, name="g_grp", align_bytes=64)
+        g_codes = keep.tile([P, 1024], U32, name="g_codes", align_bytes=64)
+        g_scl = keep.tile([P, 1024], U8, name="g_scl", align_bytes=64)
+        o_sb = keep.tile([P, 8, 512], F32, name="o_sb")
+
+        def w_rows(w):
+            return w.rearrange("(p t) k -> p t k", t=4)
+
+        def a_rows(a):
+            return a.rearrange("(p r) k -> p r k", r=8)
+
+        loads = {
+            "Whp0": (whp_raw[:, 0:2, :], w_rows(WA_hp)[:, 0:2, :]),
+            "Whp1": (whp_raw[:, 2:4, :], w_rows(WA_hp)[:, 2:4, :]),
+            "Vhp": (vhp_raw[:], w_rows(VA_hp)),
+            "Wx0": (wxp_raw[:, 0:2, :], w_rows(WA_xp)[:, 0:2, :]),
+            "Wx1": (wxp_raw[:, 2:4, :], w_rows(WA_xp)[:, 2:4, :]),
+            "Vhh": (vhh_raw[:], VA_hh.rearrange("(j p) k -> p j k", p=P)),
+        }
+        for j in range(4):
+            loads["hs%d" % j] = (hs_raw[:, 2 * j : 2 * j + 2, :], a_rows(spk_vectors)[:, 2 * j : 2 * j + 2, :])
+            loads["ha%d" % j] = (ha_raw[:, 2 * j : 2 * j + 2, :], a_rows(adr_vectors)[:, 2 * j : 2 * j + 2, :])
+            loads["x%d" % j] = (x_raw[:, 2 * j : 2 * j + 2, :], a_rows(encoder_hidden)[:, 2 * j : 2 * j + 2, :])
+
+        units = {}
+        for h in range(2):
+            units["Whp%d" % h] = (whp_raw, 2 * h, 0, w_grp[0], w_codes[0], w_scl[0], 256 * h)
+            units["Vhp%d" % h] = (vhp_raw, 2 * h, 0, w_grp[1], w_codes[1], w_scl[1], 256 * h)
+            units["Vhh%d" % h] = (vhh_raw, 2 * h, 0, w_grp[4], w_codes[4], w_scl[4], 256 * h)
+            for g in range(2):
+                units["Wx%dk%d" % (h, g)] = (wxp_raw, 2 * h, 256 * g, w_grp[2 + g], w_codes[2 + g], w_scl[2 + g], 256 * h)
+        for j in range(4):
+            units["hs%d" % j] = (hs_raw, 2 * j, 0, a_grp[0], a_codes[0], a_scl[0], 256 * j)
+            units["ha%d" % j] = (ha_raw, 2 * j, 0, a_grp[1], a_codes[1], a_scl[1], 256 * j)
+            for g in range(2):
+                units["x%dk%d" % (j, g)] = (x_raw, 2 * j, 256 * g, a_grp[2 + g], a_codes[2 + g], a_scl[2 + g], 256 * j)
+
+        live = {}
+
+        def bank(i, shape, label):
+            return psum.tile(shape, F32, tag="bank%d" % i, name=label)
+
+        def mx(dst, s, t, c0, n, start, stop):
+            nc.tensor.matmul_mx(
+                out=dst,
+                lhsT=w_codes[s][:, 128 * t : 128 * t + 128].bitcast(FP8X4),
+                lhsT_scale=w_scl[s][:, 128 * t : 128 * t + 128],
+                rhs=a_codes[s][:, c0 : c0 + n].bitcast(FP8X4),
+                rhs_scale=a_scl[s][:, c0 : c0 + n],
+                start=start,
+                stop=stop,
+            )
+
+        nc.vector.memset(warm_in[:], 0.0)
+        make_identity(nc, ident[:])
+        nc.scalar.activation(out=warm_out[:], in_=warm_in[:], func=SIGMOID)
+
+        for st in STEPS:
+            kind = st[0]
+            if kind == "L":
+                nc.sync.dma_start(out=loads[st[1]][0], in_=loads[st[1]][1])
+            elif kind == "T":
+                raw, row, w0, grp, codes, scl, c0 = units[st[1]]
+                bk = bank(st[2], [P, 2, 256], "tp_" + st[1])
+                words = raw[:].bitcast(F32)
+                for half in range(2):
+                    for i in range(2):
+                        nc.tensor.transpose(
+                            bk[:, half, 128 * i : 128 * i + 128],
+                            words[:, row + i, w0 + half : w0 + 256 : 2],
+                            ident[:],
+                        )
+                live[st[1]] = bk
+            elif kind == "C":
+                raw, row, w0, grp, codes, scl, c0 = units[st[1]]
+                src = live[st[1]][:].rearrange("p u c -> p c u")
+                if st[2] == "V":
+                    nc.vector.tensor_copy(out=grp[:, c0 : c0 + 256, :], in_=src)
+                else:
+                    nc.scalar.copy(out=grp[:, c0 : c0 + 256, :], in_=src)
+            elif kind == "Q":
+                raw, row, w0, grp, codes, scl, c0 = units[st[1]]
+                nc.vector.quantize_mx(
+                    out=codes[:, c0 : c0 + 256].bitcast(FP8X4),
+                    scales=scl[:, c0 : c0 + 256],
+                    in_=grp[:].bitcast(BF16)[:, c0 : c0 + 256, :].rearrange("p c t -> p (c t)"),
+                )
+            elif kind == "MA":
+                s = st[1]
+                if s == 0:
+                    for t in range(4):
+                        live["gate0_%d" % t] = bank(t, [P, 256], "gate0_%d" % t)
+                if s < 2:
+                    for t in range(4):
+                        mx(live["gate0_%d" % t][:], s, t, 0, 256, s == 0, False)
+                else:
+                    for t in (2 * s - 4, 2 * s - 3):
+                        mx(live["gate0_%d" % t][:], 2, t, 0, 256, False, False)
+                        mx(live["gate0_%d" % t][:], 3, t, 0, 256, False, True)
+            elif kind == "SA":
+                t = st[1]
+                nc.scalar.activation(out=sig[:, t, 0:256], in_=live["gate0_%d" % t][:], func=SIGMOID)
+            elif kind == "MB":
+                j, h = st[1], st[2]
+                bk = bank(h, [P, 2, 256], "gate%d_%d" % (j, h))
+                for i in range(2):
+                    for s in range(4):
+                        mx(bk[:, i, :], s, 2 * h + i, 256 * j, 256, s == 0, s == 3)
+                live["gate%d_%d" % (j, h)] = bk
+            elif kind == "SB":
+                j, h = st[1], st[2]
+                nc.scalar.activation(
+                    out=sig[:, 2 * h : 2 * h + 2, 256 * j : 256 * j + 256],
+                    in_=live["gate%d_%d" % (j, h)][:],
+                    func=SIGMOID,
+                )
+            elif kind == "PR":
+                c0, n = 128 * st[1], 128 * st[2]
+                nc.vector.tensor_tensor(
+                    out=g_grp[:, c0 : c0 + n, :],
+                    in0=sig[:, :, c0 : c0 + n].rearrange("p t b -> p b t"),
+                    in1=a_grp[1][:].bitcast(BF16)[:, c0 : c0 + n, :],
+                    op=MULT,
+                )
+            elif kind == "QG":
+                c0, n = 128 * st[1], 128 * st[2]
+                nc.vector.quantize_mx(
+                    out=g_codes[:, c0 : c0 + n].bitcast(FP8X4),
+                    scales=g_scl[:, c0 : c0 + n],
+                    in_=g_grp[:, c0 : c0 + n, :].rearrange("p c t -> p (c t)"),
+                )
+            elif kind == "S2":
+                r = st[1]
+                bk = bank(st[2], [P, 512], "out_%d" % r)
+                nc.tensor.matmul_mx(
+                    out=bk[:],
+                    lhsT=g_codes[:, 128 * r : 128 * r + 128].bitcast(FP8X4),
+                    lhsT_scale=g_scl[:, 128 * r : 128 * r + 128],
+                    rhs=w_codes[4][:].bitcast(FP8X4),
+                    rhs_scale=w_scl[4][:],
+                    start=True,
+                    stop=True,
+                )
+                live["out_%d" % r] = bk
+            elif kind == "OC":
+                r = st[1]
+                if st[2] == "V":
+                    nc.vector.tensor_copy(out=o_sb[:, r, :], in_=live["out_%d" % r][:])
+                else:
+                    nc.scalar.copy(out=o_sb[:, r, :], in_=live["out_%d" % r][:])
+            elif kind == "ST":
+                r0, n = st[1], st[2]
+                nc.sync.dma_start(
+                    out=out.rearrange("(p r) o -> p r o", r=8)[:, r0 : r0 + n, :], in_=o_sb[:, r0 : r0 + n, :]
+                )

@@ -13,161 +13,10 @@ MULT = mybir.AluOpType.mult
 P = 128
 FLOPS = 2 * 1024 * 512 * (1024 + 512 + 512 + 512)
 
-STEPS = [
-    ("L", "Whp0"),
-    ("L", "Whp1"),
-    ("L", "hs0"),
-    ("L", "Vhp"),
-    ("L", "ha0"),
-    ("L", "x0"),
-    ("L", "Wx0"),
-    ("L", "Wx1"),
-    ("L", "Vhh"),
-    ("L", "hs1"),
-    ("L", "ha1"),
-    ("L", "x1"),
-    ("L", "hs2"),
-    ("L", "ha2"),
-    ("L", "x2"),
-    ("L", "hs3"),
-    ("L", "ha3"),
-    ("L", "x3"),
-    ("T", "Whp0", 4),
-    ("T", "Whp1", 5),
-    ("C", "Whp0", "S"),
-    ("T", "hs0", 6),
-    ("C", "Whp1", "S"),
-    ("Q", "Whp0"),
-    ("C", "hs0", "V"),
-    ("Q", "Whp1"),
-    ("T", "Vhp0", 7),
-    ("Q", "hs0"),
-    ("T", "Vhp1", 4),
-    ("C", "Vhp0", "V"),
-    ("T", "ha0", 5),
-    ("C", "Vhp1", "S"),
-    ("MA", 0),
-    ("Q", "Vhp0"),
-    ("C", "ha0", "S"),
-    ("Q", "Vhp1"),
-    ("T", "x0k0", 6),
-    ("Q", "ha0"),
-    ("T", "x0k1", 7),
-    ("C", "x0k0", "V"),
-    ("MA", 1),
-    ("C", "x0k1", "V"),
-    ("T", "Wx0k0", 4),
-    ("Q", "x0k0"),
-    ("Q", "x0k1"),
-    ("T", "Wx0k1", 5),
-    ("C", "Wx0k0", "V"),
-    ("T", "Wx1k0", 6),
-    ("C", "Wx0k1", "S"),
-    ("T", "Wx1k1", 7),
-    ("Q", "Wx0k0"),
-    ("C", "Wx1k0", "V"),
-    ("T", "Vhh0", 4),
-    ("T", "Vhh1", 5),
-    ("Q", "Wx0k1"),
-    ("T", "hs1", 6),
-    ("Q", "Wx1k0"),
-    ("C", "Vhh1", "S"),
-    ("C", "Wx1k1", "V"),
-    ("MA", 2),
-    ("C", "Vhh0", "V"),
-    ("T", "ha1", 7),
-    ("SA", 0),
-    ("Q", "Wx1k1"),
-    ("SA", 1),
-    ("T", "x1k0", 4),
-    ("Q", "Vhh0"),
-    ("Q", "Vhh1"),
-    ("T", "x1k1", 5),
-    ("C", "hs1", "V"),
-    ("C", "x1k0", "S"),
-    ("MA", 3),
-    ("C", "ha1", "V"),
-    ("C", "x1k1", "S"),
-    ("T", "hs2", 6),
-    ("Q", "hs1"),
-    ("SA", 2),
-    ("T", "ha2", 7),
-    ("Q", "ha1"),
-    ("C", "hs2", "S"),
-    ("Q", "x1k0"),
-    ("T", "x2k0", 4),
-    ("Q", "x1k1"),
-    ("SA", 3),
-    ("T", "x2k1", 5),
-    ("Q", "hs2"),
-    ("C", "x2k0", "S"),
-    ("T", "hs3", 6),
-    ("C", "ha2", "V"),
-    ("MB", 1, 0),
-    ("C", "hs3", "S"),
-    ("Q", "x2k0"),
-    ("Q", "ha2"),
-    ("C", "x2k1", "V"),
-    ("MB", 1, 1),
-    ("SB", 1, 0),
-    ("Q", "hs3"),
-    ("Q", "x2k1"),
-    ("PR", 0, 1),
-    ("T", "ha3", 7),
-    ("SB", 1, 1),
-    ("T", "x3k0", 4),
-    ("QG", 0, 1),
-    ("PR", 1, 1),
-    ("T", "x3k1", 5),
-    ("C", "ha3", "S"),
-    ("S2", 0, 2),
-    ("QG", 1, 1),
-    ("C", "x3k0", "S"),
-    ("MB", 2, 0),
-    ("Q", "ha3"),
-    ("C", "x3k1", "S"),
-    ("Q", "x3k0"),
-    ("OC", 0, "S"),
-    ("S2", 1, 3),
-    ("Q", "x3k1"),
-    ("MB", 2, 1),
-    ("SB", 2, 0),
-    ("OC", 1, "V"),
-    ("PR", 2, 1),
-    ("ST", 0, 2),
-    ("MB", 3, 0),
-    ("SB", 2, 1),
-    ("QG", 2, 1),
-    ("PR", 3, 1),
-    ("S2", 2, 2),
-    ("QG", 3, 1),
-    ("PR", 4, 1),
-    ("MB", 3, 1),
-    ("SB", 3, 0),
-    ("OC", 2, "S"),
-    ("QG", 4, 1),
-    ("PR", 5, 1),
-    ("S2", 3, 3),
-    ("S2", 4, 2),
-    ("SB", 3, 1),
-    ("QG", 5, 1),
-    ("OC", 3, "V"),
-    ("OC", 4, "S"),
-    ("PR", 6, 1),
-    ("ST", 2, 2),
-    ("S2", 5, 3),
-    ("QG", 6, 1),
-    ("OC", 5, "S"),
-    ("PR", 7, 1),
-    ("S2", 6, 2),
-    ("ST", 4, 2),
-    ("QG", 7, 1),
-    ("OC", 6, "S"),
-    ("S2", 7, 3),
-    ("OC", 7, "S"),
-    ("ST", 6, 1),
-    ("ST", 7, 1),
-]
+PAIRS = [[["Whp",0,0],["Whp",1,0]],[["hs",0,0],["ha",0,0]],[["Vhp",0,0],["Vhp",1,0]],[["x",0,0],["x",0,1]],[["Wx",0,0],["Wx",0,1]],[["Wx",1,0],["Wx",1,1]],[["hs",1,0],["ha",1,0]],[["x",1,0],["x",1,1]],[["Vhh",0,0],["Vhh",1,0]],[["hs",2,0],["ha",2,0]],[["x",2,0],["x",2,1]],[["hs",3,0],["ha",3,0]],[["x",3,0],["x",3,1]]]
+LOADS = [["Whp",0,2],["Whp",2,2],["hs",0,2],["ha",0,2],["Vhp",0,4],["x",0,2],["Wx",0,2],["Wx",2,2],["hs",2,2],["ha",2,2],["x",2,2],["Vhh",0,4],["hs",4,2],["ha",4,2],["x",4,2],["hs",6,2],["ha",6,2],["x",6,2]]
+PERMUTED = [["x",1,0],["x",1,1],["Vhh",0,0],["Vhh",1,0],["hs",2,0],["ha",2,0],["x",2,0],["x",2,1],["hs",3,0],["ha",3,0],["x",3,0],["x",3,1]]
+VECTOR_DRAWS = []
 
 
 def tile_updatespeaker_pa_kernel(
@@ -176,179 +25,253 @@ def tile_updatespeaker_pa_kernel(
     nc = tc.nc
     with ExitStack() as ctx:
         keep = ctx.enter_context(tc.tile_pool(name="keep", bufs=1))
-        psum = ctx.enter_context(tc.psum_pool(name="psum", bufs=1))
+        flips = ctx.enter_context(tc.psum_pool(name="flips", bufs=4))
+        gates = ctx.enter_context(tc.psum_pool(name="gates", bufs=2))
+        outs = ctx.enter_context(tc.psum_pool(name="outs", bufs=2))
 
         ident = keep.tile([P, P], F32, name="ident")
         warm_in = keep.tile([P, 1], F32, name="warm_in")
         warm_out = keep.tile([P, 1], F32, name="warm_out")
 
-        whp_raw = keep.tile([P, 4, 512], BF16, name="whp_raw")
-        vhp_raw = keep.tile([P, 4, 512], BF16, name="vhp_raw")
-        vhh_raw = keep.tile([P, 4, 512], BF16, name="vhh_raw")
-        wxp_raw = keep.tile([P, 4, 1024], BF16, name="wxp_raw")
-        hs_raw = keep.tile([P, 8, 512], BF16, name="hs_raw")
-        ha_raw = keep.tile([P, 8, 512], BF16, name="ha_raw")
-        x_raw = keep.tile([P, 8, 1024], BF16, name="x_raw")
+        raw = {}
+        for name, rows, width in (
+            ("Whp", 4, 512), ("Vhp", 4, 512), ("Vhh", 4, 512), ("Wx", 4, 1024), ("hs", 8, 512), ("ha", 8, 512), ("x", 8, 1024)
+        ):
+            raw[name] = keep.tile([P, rows, width], BF16, name=name + "_raw")
 
-        w_grp = [keep.tile([P, 512, 2], F32, name="w_grp%d" % s, align_bytes=64) for s in range(5)]
-        w_codes = [keep.tile([P, 512], U32, name="w_codes%d" % s, align_bytes=64) for s in range(5)]
-        w_scl = [keep.tile([P, 512], U8, name="w_scl%d" % s, align_bytes=64) for s in range(5)]
-        a_grp = [keep.tile([P, 1024, 2], F32, name="a_grp%d" % s, align_bytes=64) for s in range(4)]
-        a_codes = [keep.tile([P, 1024], U32, name="a_codes%d" % s, align_bytes=64) for s in range(4)]
-        a_scl = [keep.tile([P, 1024], U8, name="a_scl%d" % s, align_bytes=64) for s in range(4)]
-        sig = keep.tile([P, 4, 1024], F32, name="sig")
+        hbm = {
+            "Whp": WA_hp.rearrange("(p t) k -> p t k", t=4),
+            "Vhp": VA_hp.rearrange("(p t) k -> p t k", t=4),
+            "Wx": WA_xp.rearrange("(p t) k -> p t k", t=4),
+            "Vhh": VA_hh.rearrange("(j p) k -> p j k", p=P),
+            "hs": spk_vectors.rearrange("(p r) k -> p r k", r=8),
+            "ha": adr_vectors.rearrange("(p r) k -> p r k", r=8),
+            "x": encoder_hidden.rearrange("(p r) k -> p r k", r=8),
+        }
+
+        grp = {}
+        codes = {}
+        scl = {}
+        for name, width in (
+            ("Whp", 512), ("Vhp", 512), ("Wxk0", 512), ("Wxk1", 512), ("Vhh", 512),
+            ("hs", 1024), ("ha", 1024), ("xk0", 1024), ("xk1", 1024),
+        ):
+            grp[name] = keep.tile([P, width, 2], F32, name="grp_" + name, align_bytes=64)
+            codes[name] = keep.tile([P, width], U32, name="codes_" + name, align_bytes=64)
+            scl[name] = keep.tile([P, width], U8, name="scl_" + name, align_bytes=64)
         g_grp = keep.tile([P, 1024, 4], BF16, name="g_grp", align_bytes=64)
         g_codes = keep.tile([P, 1024], U32, name="g_codes", align_bytes=64)
         g_scl = keep.tile([P, 1024], U8, name="g_scl", align_bytes=64)
+        sig = keep.tile([P, 4, 1024], F32, name="sig")
         o_sb = keep.tile([P, 8, 512], F32, name="o_sb")
 
-        def w_rows(w):
-            return w.rearrange("(p t) k -> p t k", t=4)
+        def load(name, r0, n):
+            nc.sync.dma_start(out=raw[name][:, r0 : r0 + n, :], in_=hbm[name][:, r0 : r0 + n, :])
 
-        def a_rows(a):
-            return a.rearrange("(p r) k -> p r k", r=8)
-
-        loads = {
-            "Whp0": (whp_raw[:, 0:2, :], w_rows(WA_hp)[:, 0:2, :]),
-            "Whp1": (whp_raw[:, 2:4, :], w_rows(WA_hp)[:, 2:4, :]),
-            "Vhp": (vhp_raw[:], w_rows(VA_hp)),
-            "Wx0": (wxp_raw[:, 0:2, :], w_rows(WA_xp)[:, 0:2, :]),
-            "Wx1": (wxp_raw[:, 2:4, :], w_rows(WA_xp)[:, 2:4, :]),
-            "Vhh": (vhh_raw[:], VA_hh.rearrange("(j p) k -> p j k", p=P)),
-        }
-        for j in range(4):
-            loads["hs%d" % j] = (hs_raw[:, 2 * j : 2 * j + 2, :], a_rows(spk_vectors)[:, 2 * j : 2 * j + 2, :])
-            loads["ha%d" % j] = (ha_raw[:, 2 * j : 2 * j + 2, :], a_rows(adr_vectors)[:, 2 * j : 2 * j + 2, :])
-            loads["x%d" % j] = (x_raw[:, 2 * j : 2 * j + 2, :], a_rows(encoder_hidden)[:, 2 * j : 2 * j + 2, :])
-
-        units = {}
-        for h in range(2):
-            units["Whp%d" % h] = (whp_raw, 2 * h, 0, w_grp[0], w_codes[0], w_scl[0], 256 * h)
-            units["Vhp%d" % h] = (vhp_raw, 2 * h, 0, w_grp[1], w_codes[1], w_scl[1], 256 * h)
-            units["Vhh%d" % h] = (vhh_raw, 2 * h, 0, w_grp[4], w_codes[4], w_scl[4], 256 * h)
-            for g in range(2):
-                units["Wx%dk%d" % (h, g)] = (wxp_raw, 2 * h, 256 * g, w_grp[2 + g], w_codes[2 + g], w_scl[2 + g], 256 * h)
-        for j in range(4):
-            units["hs%d" % j] = (hs_raw, 2 * j, 0, a_grp[0], a_codes[0], a_scl[0], 256 * j)
-            units["ha%d" % j] = (ha_raw, 2 * j, 0, a_grp[1], a_codes[1], a_scl[1], 256 * j)
-            for g in range(2):
-                units["x%dk%d" % (j, g)] = (x_raw, 2 * j, 256 * g, a_grp[2 + g], a_codes[2 + g], a_scl[2 + g], 256 * j)
+        def parts(unit):
+            name, i, g = unit
+            dst = name + "k%d" % g if name in ("x", "Wx") else name
+            return name, 2 * i, 256 * g, dst, 256 * i
 
         live = {}
+        count = [0]
+        perm = {}
 
-        def bank(i, shape, label):
-            return psum.tile(shape, F32, tag="bank%d" % i, name=label)
+        def flip(unit):
+            name, row, w0, dst, c0 = parts(unit)
+            label = "%s_%d_%d" % (name, row, w0)
+            words = raw[name][:].bitcast(F32)
+            bank = flips.tile([P, 2, 256], F32, tag="flip", name="flip_" + label)
+            if unit in PERMUTED:
+                pm = perm[tuple(unit)]
+            for half in range(2):
+                for i in range(2):
+                    if unit in PERMUTED:
+                        src = pm[:, i, half, :]
+                    else:
+                        src = words[:, row + i, w0 + half : w0 + 256 : 2]
+                    nc.tensor.transpose(bank[:, half, 128 * i : 128 * i + 128], src, ident[:])
+            live[label] = bank
 
-        def mx(dst, s, t, c0, n, start, stop):
+        def permute(unit):
+            if unit not in PERMUTED:
+                return
+            name, row, w0, dst, c0 = parts(unit)
+            label = "%s_%d_%d" % (name, row, w0)
+            words = raw[name][:].bitcast(F32)
+            pm = keep.tile([P, 2, 2, 128], F32, name="perm_" + label)
+            perm[tuple(unit)] = pm
+            nc.vector.tensor_copy(
+                out=pm[:], in_=words[:, row : row + 2, w0 : w0 + 256].rearrange("p r (m u) -> p r u m", u=2)
+            )
+
+        def draw(unit):
+            name, row, w0, dst, c0 = parts(unit)
+            label = "%s_%d_%d" % (name, row, w0)
+            src = live[label][:].rearrange("p u c -> p c u")
+            if unit in VECTOR_DRAWS:
+                nc.vector.tensor_copy(out=grp[dst][:, c0 : c0 + 256, :], in_=src)
+            else:
+                nc.scalar.copy(out=grp[dst][:, c0 : c0 + 256, :], in_=src)
+
+        def quant(unit):
+            name, row, w0, dst, c0 = parts(unit)
+            nc.vector.quantize_mx(
+                out=codes[dst][:, c0 : c0 + 256].bitcast(FP8X4),
+                scales=scl[dst][:, c0 : c0 + 256],
+                in_=grp[dst][:].bitcast(BF16)[:, c0 : c0 + 256, :].rearrange("p c t -> p (c t)"),
+            )
+
+        SUMS = (("Whp", "hs"), ("Vhp", "ha"), ("Wxk0", "xk0"), ("Wxk1", "xk1"))
+
+        def gate_sum(dst, t, c0, n):
+            for s, (w, a) in enumerate(SUMS):
+                nc.tensor.matmul_mx(
+                    out=dst,
+                    lhsT=codes[w][:, 128 * t : 128 * t + 128].bitcast(FP8X4),
+                    lhsT_scale=scl[w][:, 128 * t : 128 * t + 128],
+                    rhs=codes[a][:, c0 : c0 + n].bitcast(FP8X4),
+                    rhs_scale=scl[a][:, c0 : c0 + n],
+                    start=s == 0,
+                    stop=s == 3,
+                )
+
+        def gate(j, h):
+            bank = gates.tile([P, 2, 256], F32, tag="gate", name="gate_%d_%d" % (j, h))
+            for i in range(2):
+                gate_sum(bank[:, i, :], 2 * h + i, 256 * j, 256)
+            live["gate_%d_%d" % (j, h)] = bank
+
+        def sigm(j, h):
+            nc.scalar.activation(
+                out=sig[:, 2 * h : 2 * h + 2, 256 * j : 256 * j + 256], in_=live["gate_%d_%d" % (j, h)][:], func=SIGMOID
+            )
+
+        def gate_rows(r):
+            bank = gates.tile([P, 4, 128], F32, tag="gate", name="gate_r%d" % r)
+            for t in range(4):
+                gate_sum(bank[:, t, :], t, 128 * r, 128)
+            live["gate_r%d" % r] = bank
+
+        def sigm_rows(r):
+            nc.scalar.activation(out=sig[:, :, 128 * r : 128 * r + 128], in_=live["gate_r%d" % r][:], func=SIGMOID)
+
+        def prod(r):
+            nc.vector.tensor_tensor(
+                out=g_grp[:, 128 * r : 128 * r + 128, :],
+                in0=sig[:, :, 128 * r : 128 * r + 128].rearrange("p t b -> p b t"),
+                in1=grp["ha"][:].bitcast(BF16)[:, 128 * r : 128 * r + 128, :],
+                op=MULT,
+            )
+
+        def quantg(r):
+            nc.vector.quantize_mx(
+                out=g_codes[:, 128 * r : 128 * r + 128].bitcast(FP8X4),
+                scales=g_scl[:, 128 * r : 128 * r + 128],
+                in_=g_grp[:, 128 * r : 128 * r + 128, :].rearrange("p c t -> p (c t)"),
+            )
+
+        def project(r):
+            bank = outs.tile([P, 512], F32, tag="out", name="out_%d" % r)
             nc.tensor.matmul_mx(
-                out=dst,
-                lhsT=w_codes[s][:, 128 * t : 128 * t + 128].bitcast(FP8X4),
-                lhsT_scale=w_scl[s][:, 128 * t : 128 * t + 128],
-                rhs=a_codes[s][:, c0 : c0 + n].bitcast(FP8X4),
-                rhs_scale=a_scl[s][:, c0 : c0 + n],
-                start=start,
-                stop=stop,
+                out=bank[:],
+                lhsT=g_codes[:, 128 * r : 128 * r + 128].bitcast(FP8X4),
+                lhsT_scale=g_scl[:, 128 * r : 128 * r + 128],
+                rhs=codes["Vhh"][:].bitcast(FP8X4),
+                rhs_scale=scl["Vhh"][:],
+                start=True,
+                stop=True,
+            )
+            live["out_%d" % r] = bank
+
+        def evac(r, eng):
+            if eng == "V":
+                nc.vector.tensor_copy(out=o_sb[:, r, :], in_=live["out_%d" % r][:])
+            else:
+                nc.scalar.copy(out=o_sb[:, r, :], in_=live["out_%d" % r][:])
+
+        def store(r0, n):
+            nc.sync.dma_start(
+                out=out.rearrange("(p r) o -> p r o", r=8)[:, r0 : r0 + n, :], in_=o_sb[:, r0 : r0 + n, :]
             )
 
         nc.vector.memset(warm_in[:], 0.0)
         make_identity(nc, ident[:])
         nc.scalar.activation(out=warm_out[:], in_=warm_in[:], func=SIGMOID)
+        for name, r0, n in LOADS:
+            load(name, r0, n)
+        ctx.enter_context(tc.manual_schedule())
 
-        for st in STEPS:
-            kind = st[0]
-            if kind == "L":
-                nc.sync.dma_start(out=loads[st[1]][0], in_=loads[st[1]][1])
-            elif kind == "T":
-                raw, row, w0, grp, codes, scl, c0 = units[st[1]]
-                bk = bank(st[2], [P, 2, 256], "tp_" + st[1])
-                words = raw[:].bitcast(F32)
-                for half in range(2):
-                    for i in range(2):
-                        nc.tensor.transpose(
-                            bk[:, half, 128 * i : 128 * i + 128],
-                            words[:, row + i, w0 + half : w0 + 256 : 2],
-                            ident[:],
-                        )
-                live[st[1]] = bk
-            elif kind == "C":
-                raw, row, w0, grp, codes, scl, c0 = units[st[1]]
-                src = live[st[1]][:].rearrange("p u c -> p c u")
-                if st[2] == "V":
-                    nc.vector.tensor_copy(out=grp[:, c0 : c0 + 256, :], in_=src)
-                else:
-                    nc.scalar.copy(out=grp[:, c0 : c0 + 256, :], in_=src)
-            elif kind == "Q":
-                raw, row, w0, grp, codes, scl, c0 = units[st[1]]
-                nc.vector.quantize_mx(
-                    out=codes[:, c0 : c0 + 256].bitcast(FP8X4),
-                    scales=scl[:, c0 : c0 + 256],
-                    in_=grp[:].bitcast(BF16)[:, c0 : c0 + 256, :].rearrange("p c t -> p (c t)"),
-                )
-            elif kind == "MA":
-                s = st[1]
-                if s == 0:
-                    for t in range(4):
-                        live["gate0_%d" % t] = bank(t, [P, 256], "gate0_%d" % t)
-                if s < 2:
-                    for t in range(4):
-                        mx(live["gate0_%d" % t][:], s, t, 0, 256, s == 0, False)
-                else:
-                    for t in (2 * s - 4, 2 * s - 3):
-                        mx(live["gate0_%d" % t][:], 2, t, 0, 256, False, False)
-                        mx(live["gate0_%d" % t][:], 3, t, 0, 256, False, True)
-            elif kind == "SA":
-                t = st[1]
-                nc.scalar.activation(out=sig[:, t, 0:256], in_=live["gate0_%d" % t][:], func=SIGMOID)
-            elif kind == "MB":
-                j, h = st[1], st[2]
-                bk = bank(h, [P, 2, 256], "gate%d_%d" % (j, h))
-                for i in range(2):
-                    for s in range(4):
-                        mx(bk[:, i, :], s, 2 * h + i, 256 * j, 256, s == 0, s == 3)
-                live["gate%d_%d" % (j, h)] = bk
-            elif kind == "SB":
-                j, h = st[1], st[2]
-                nc.scalar.activation(
-                    out=sig[:, 2 * h : 2 * h + 2, 256 * j : 256 * j + 256],
-                    in_=live["gate%d_%d" % (j, h)][:],
-                    func=SIGMOID,
-                )
-            elif kind == "PR":
-                c0, n = 128 * st[1], 128 * st[2]
-                nc.vector.tensor_tensor(
-                    out=g_grp[:, c0 : c0 + n, :],
-                    in0=sig[:, :, c0 : c0 + n].rearrange("p t b -> p b t"),
-                    in1=a_grp[1][:].bitcast(BF16)[:, c0 : c0 + n, :],
-                    op=MULT,
-                )
-            elif kind == "QG":
-                c0, n = 128 * st[1], 128 * st[2]
-                nc.vector.quantize_mx(
-                    out=g_codes[:, c0 : c0 + n].bitcast(FP8X4),
-                    scales=g_scl[:, c0 : c0 + n],
-                    in_=g_grp[:, c0 : c0 + n, :].rearrange("p c t -> p (c t)"),
-                )
-            elif kind == "S2":
-                r = st[1]
-                bk = bank(st[2], [P, 512], "out_%d" % r)
-                nc.tensor.matmul_mx(
-                    out=bk[:],
-                    lhsT=g_codes[:, 128 * r : 128 * r + 128].bitcast(FP8X4),
-                    lhsT_scale=g_scl[:, 128 * r : 128 * r + 128],
-                    rhs=w_codes[4][:].bitcast(FP8X4),
-                    rhs_scale=w_scl[4][:],
-                    start=True,
-                    stop=True,
-                )
-                live["out_%d" % r] = bk
-            elif kind == "OC":
-                r = st[1]
-                if st[2] == "V":
-                    nc.vector.tensor_copy(out=o_sb[:, r, :], in_=live["out_%d" % r][:])
-                else:
-                    nc.scalar.copy(out=o_sb[:, r, :], in_=live["out_%d" % r][:])
-            elif kind == "ST":
-                r0, n = st[1], st[2]
-                nc.sync.dma_start(
-                    out=out.rearrange("(p r) o -> p r o", r=8)[:, r0 : r0 + n, :], in_=o_sb[:, r0 : r0 + n, :]
-                )
+
+        def prep(k):
+            if k < 12:
+                for u in PAIRS[k + 1]:
+                    permute(u)
+            for u in PAIRS[k]:
+                flip(u)
+            for u in PAIRS[k]:
+                draw(u)
+            for u in PAIRS[k]:
+                quant(u)
+
+        for k in range(7):
+            prep(k)
+        gate(0, 0)
+        prep(7)
+        sigm(0, 0)
+        gate(0, 1)
+        prep(8)
+        sigm(0, 1)
+        prep(9)
+        gate(1, 0)
+        prod(0)
+        sigm(1, 0)
+        prod(1)
+        quantg(0)
+        prep(10)
+        quantg(1)
+        gate(1, 1)
+        sigm(1, 1)
+        prep(11)
+        prod(2)
+        project(0)
+        prep(12)
+        prod(3)
+        quantg(2)
+        gate(2, 0)
+        quantg(3)
+        evac(0, "S")
+        sigm(2, 0)
+        project(1)
+        gate(2, 1)
+        evac(1, "V")
+        sigm(2, 1)
+        store(0, 2)
+        project(2)
+        project(3)
+        gate_rows(6)
+        prod(4)
+        evac(2, "S")
+        prod(5)
+        quantg(4)
+        sigm_rows(6)
+        evac(3, "V")
+        quantg(5)
+        store(2, 2)
+        gate_rows(7)
+        prod(6)
+        sigm_rows(7)
+        project(4)
+        quantg(6)
+        evac(4, "S")
+        project(5)
+        prod(7)
+        evac(5, "S")
+        store(4, 2)
+        project(6)
+        quantg(7)
+        evac(6, "V")
+        store(6, 1)
+        project(7)
+        evac(7, "S")
+        store(7, 1)

@@ -15,7 +15,7 @@ FLOPS = 2 * 1024 * 512 * (1024 + 512 + 512 + 512)
 
 PAIRS = [[["Whp",0,0],["Whp",1,0]],[["hs",0,0],["ha",0,0]],[["Vhp",0,0],["Vhp",1,0]],[["x",0,0],["x",0,1]],[["Wx",0,0],["Wx",0,1]],[["Wx",1,0],["Wx",1,1]],[["hs",1,0],["ha",1,0]],[["x",1,0],["x",1,1]],[["Vhh",0,0],["Vhh",1,0]],[["hs",2,0],["ha",2,0]],[["x",2,0],["x",2,1]],[["hs",3,0],["ha",3,0]],[["x",3,0],["x",3,1]]]
 LOADS = [["Whp",0,2],["Whp",2,2],["hs",0,2],["ha",0,2],["Vhp",0,4],["x",0,2],["Wx",0,2],["Wx",2,2],["hs",2,2],["ha",2,2],["x",2,2],["Vhh",0,4],["hs",4,2],["ha",4,2],["x",4,2],["hs",6,2],["ha",6,2],["x",6,2]]
-PERMUTED = [["x",1,0],["x",1,1],["Vhh",0,0],["Vhh",1,0],["hs",2,0],["ha",2,0],["x",2,0],["x",2,1],["hs",3,0],["ha",3,0],["x",3,0],["x",3,1]]
+PERMUTED = []
 VECTOR_DRAWS = []
 
 

@@ -16,7 +16,7 @@ FLOPS = 2 * 1024 * 512 * (1024 + 512 + 512 + 512)
 PAIRS = [[["Whp",0,0],["Whp",1,0]],[["hs",0,0],["ha",0,0]],[["Vhp",0,0],["Vhp",1,0]],[["x",0,0],["x",0,1]],[["Wx",0,0],["Wx",0,1]],[["Wx",1,0],["Wx",1,1]],[["hs",1,0],["ha",1,0]],[["x",1,0],["x",1,1]],[["Vhh",0,0],["Vhh",1,0]],[["hs",2,0],["ha",2,0]],[["x",2,0],["x",2,1]],[["hs",3,0],["ha",3,0]],[["x",3,0],["x",3,1]]]
 LOADS = [["Whp",0,2],["Whp",2,2],["hs",0,2],["ha",0,2],["Vhp",0,4],["x",0,2],["Wx",0,2],["Wx",2,2],["hs",2,2],["ha",2,2],["x",2,2],["Vhh",0,4],["hs",4,2],["ha",4,2],["x",4,2],["hs",6,2],["ha",6,2],["x",6,2]]
 PERMUTED = []
-VECTOR_DRAWS = []
+VECTOR_DRAWS = [["hs",0,0],["Vhp",1,0],["Wx",0,0],["Wx",1,1],["x",1,0],["Vhh",1,0],["x",2,0],["ha",3,0]]
 
 
 def tile_updatespeaker_pa_kernel(

@@ -14,7 +14,7 @@ P = 128
 FLOPS = 2 * 1024 * 512 * (1024 + 512 + 512 + 512)
 
 PAIRS = [[["Whp",0,0],["Whp",1,0]],[["hs",0,0],["ha",0,0]],[["Vhp",0,0],["Vhp",1,0]],[["x",0,0],["x",0,1]],[["Wx",0,0],["Wx",0,1]],[["Wx",1,0],["Wx",1,1]],[["hs",1,0],["ha",1,0]],[["x",1,0],["x",1,1]],[["Vhh",0,0],["Vhh",1,0]],[["hs",2,0],["ha",2,0]],[["x",2,0],["x",2,1]],[["hs",3,0],["ha",3,0]],[["x",3,0],["x",3,1]]]
-LOADS = [["Whp",0,2],["Whp",2,2],["hs",0,2],["ha",0,2],["Vhp",0,4],["x",0,2],["Wx",0,2],["Wx",2,2],["hs",2,2],["ha",2,2],["x",2,2],["Vhh",0,4],["hs",4,2],["ha",4,2],["x",4,2],["hs",6,2],["ha",6,2],["x",6,2]]
+LOADS = [["Whp",0,2],["Whp",2,2],["hs",0,2],["ha",0,2],["Vhp",0,2],["Vhp",2,2],["x",0,2],["Wx",0,2],["Wx",2,2],["hs",2,2],["ha",2,2],["x",2,2],["Vhh",0,4],["hs",4,2],["ha",4,2],["x",4,2],["hs",6,2],["ha",6,2],["x",6,2]]
 PERMUTED = []
 VECTOR_DRAWS = [["hs",0,0],["Vhp",1,0],["Wx",0,0],["Wx",1,1],["x",1,0],["Vhh",1,0],["x",2,0],["ha",3,0]]
 
@@ -84,8 +84,8 @@ def tile_updatespeaker_pa_kernel(
             bank = flips.tile([P, 2, 256], F32, tag="flip", name="flip_" + label)
             if unit in PERMUTED:
                 pm = perm[tuple(unit)]
-            for half in range(2):
-                for i in range(2):
+            for i in range(2):
+                for half in range(2):
                     if unit in PERMUTED:
                         src = pm[:, i, half, :]
                     else:
@@ -153,6 +153,19 @@ def tile_updatespeaker_pa_kernel(
                 gate_sum(bank[:, t, :], t, 128 * r, 128)
             live["gate_r%d" % r] = bank
 
+        def gate_rows_split(r):
+            for h in range(2):
+                bank = flips.tile([P, 2, 128], F32, tag="flip", name="gate_r%d_%d" % (r, h))
+                for i in range(2):
+                    gate_sum(bank[:, i, :], 2 * h + i, 128 * r, 128)
+                live["gate_r%d_%d" % (r, h)] = bank
+
+        def sigm_rows_split(r):
+            for h in range(2):
+                nc.scalar.activation(
+                    out=sig[:, 2 * h : 2 * h + 2, 128 * r : 128 * r + 128], in_=live["gate_r%d_%d" % (r, h)][:], func=SIGMOID
+                )
+
         def sigm_rows(r):
             nc.scalar.activation(out=sig[:, :, 128 * r : 128 * r + 128], in_=live["gate_r%d" % r][:], func=SIGMOID)
 
@@ -172,7 +185,7 @@ def tile_updatespeaker_pa_kernel(
             )
 
         def project(r):
-            bank = outs.tile([P, 512], F32, tag="out", name="out_%d" % r)
+            bank = flips.tile([P, 512], F32, tag="flip", name="out_%d" % r) if r in [2,3,5] else outs.tile([P, 512], F32, tag="out", name="out_%d" % r)
             nc.tensor.matmul_mx(
                 out=bank[:],
                 lhsT=g_codes[:, 128 * r : 128 * r + 128].bitcast(FP8X4),
@@ -185,10 +198,41 @@ def tile_updatespeaker_pa_kernel(
             live["out_%d" % r] = bank
 
         def evac(r, eng):
+            src = live["out_%d" % r][:]
+            dst = o_sb[:, r, :]
             if eng == "V":
-                nc.vector.tensor_copy(out=o_sb[:, r, :], in_=live["out_%d" % r][:])
+                nc.vector.tensor_copy(out=dst, in_=src)
             else:
-                nc.scalar.copy(out=o_sb[:, r, :], in_=live["out_%d" % r][:])
+                nc.scalar.copy(out=dst, in_=src)
+
+        def project_halves(r):
+            for h in range(2):
+                bank = (outs if h else flips).tile([P, 256], F32, tag="out" if h else "flip", name="out_%d_%d" % (r, h))
+                nc.tensor.matmul_mx(
+                    out=bank[:],
+                    lhsT=g_codes[:, 128 * r : 128 * r + 128].bitcast(FP8X4),
+                    lhsT_scale=g_scl[:, 128 * r : 128 * r + 128],
+                    rhs=codes["Vhh"][:, 256 * h : 256 * h + 256].bitcast(FP8X4),
+                    rhs_scale=scl["Vhh"][:, 256 * h : 256 * h + 256],
+                    start=True,
+                    stop=True,
+                )
+                live["out_%d_%d" % (r, h)] = bank
+
+        def evac_halves(r):
+            for h in range(2):
+                src = live["out_%d_%d" % (r, h)][:]
+                dst = o_sb[:, r, 256 * h : 256 * h + 256]
+                if h:
+                    nc.scalar.copy(out=dst, in_=src)
+                else:
+                    nc.vector.tensor_copy(out=dst, in_=src)
+
+        def store_half(r, h):
+            nc.sync.dma_start(
+                out=out.rearrange("(p r) o -> p r o", r=8)[:, r, 256 * h : 256 * h + 256],
+                in_=o_sb[:, r, 256 * h : 256 * h + 256],
+            )
 
         def store(r0, n):
             nc.sync.dma_start(
@@ -204,7 +248,7 @@ def tile_updatespeaker_pa_kernel(
 
 
         def prep(k):
-            if k < 12:
+            if k + 1 < 13:
                 for u in PAIRS[k + 1]:
                     permute(u)
             for u in PAIRS[k]:
@@ -213,7 +257,6 @@ def tile_updatespeaker_pa_kernel(
                 draw(u)
             for u in PAIRS[k]:
                 quant(u)
-
         for k in range(7):
             prep(k)
         gate(0, 0)
@@ -254,24 +297,26 @@ def tile_updatespeaker_pa_kernel(
         evac(2, "S")
         prod(5)
         quantg(4)
+        evac(3, "S")
         sigm_rows(6)
-        evac(3, "V")
         quantg(5)
         store(2, 2)
-        gate_rows(7)
+        gate_rows_split(7)
         prod(6)
-        sigm_rows(7)
+        sigm_rows_split(7)
         project(4)
         quantg(6)
         evac(4, "S")
+        store(4, 1)
         project(5)
         prod(7)
         evac(5, "S")
-        store(4, 2)
+        store(5, 1)
         project(6)
         quantg(7)
         evac(6, "V")
         store(6, 1)
-        project(7)
-        evac(7, "S")
-        store(7, 1)
+        project_halves(7)
+        evac_halves(7)
+        store_half(7, 0)
+        store_half(7, 1)

@@ -26,8 +26,7 @@ def tile_updatespeaker_pa_kernel(
     with ExitStack() as ctx:
         keep = ctx.enter_context(tc.tile_pool(name="keep", bufs=1))
         flips = ctx.enter_context(tc.psum_pool(name="flips", bufs=4))
-        gates = ctx.enter_context(tc.psum_pool(name="gates", bufs=2))
-        outs = ctx.enter_context(tc.psum_pool(name="outs", bufs=2))
+        acc = ctx.enter_context(tc.psum_pool(name="acc", bufs=1))
 
         ident = keep.tile([P, P], F32, name="ident")
         warm_in = keep.tile([P, 1], F32, name="warm_in")
@@ -136,8 +135,26 @@ def tile_updatespeaker_pa_kernel(
                     stop=s == 3,
                 )
 
+        def first_pass(s):
+            w, a = SUMS[s]
+            for t in range(4):
+                if s == 0:
+                    live["first_%d" % t] = acc.tile([P, 256], F32, tag="acc%d" % t, name="first_%d" % t)
+                nc.tensor.matmul_mx(
+                    out=live["first_%d" % t][:],
+                    lhsT=codes[w][:, 128 * t : 128 * t + 128].bitcast(FP8X4),
+                    lhsT_scale=scl[w][:, 128 * t : 128 * t + 128],
+                    rhs=codes[a][:, 0:256].bitcast(FP8X4),
+                    rhs_scale=scl[a][:, 0:256],
+                    start=s == 0,
+                    stop=s == 3,
+                )
+
+        def first_sigm(t):
+            nc.scalar.activation(out=sig[:, t, 0:256], in_=live["first_%d" % t][:], func=SIGMOID)
+
         def gate(j, h):
-            bank = gates.tile([P, 2, 256], F32, tag="gate", name="gate_%d_%d" % (j, h))
+            bank = acc.tile([P, 2, 256], F32, tag="acc%d" % h, name="gate_%d_%d" % (j, h))
             for i in range(2):
                 gate_sum(bank[:, i, :], 2 * h + i, 256 * j, 256)
             live["gate_%d_%d" % (j, h)] = bank
@@ -148,20 +165,20 @@ def tile_updatespeaker_pa_kernel(
             )
 
         def gate_rows(r):
-            bank = gates.tile([P, 4, 128], F32, tag="gate", name="gate_r%d" % r)
+            bank = acc.tile([P, 4, 128], F32, tag="acc%d" % (r % 2), name="gate_r%d" % r)
             for t in range(4):
                 gate_sum(bank[:, t, :], t, 128 * r, 128)
             live["gate_r%d" % r] = bank
 
-        def gate_rows_split(r):
-            for h in range(2):
+        def gate_rows_split(r, hs=(0, 1)):
+            for h in hs:
                 bank = flips.tile([P, 2, 128], F32, tag="flip", name="gate_r%d_%d" % (r, h))
                 for i in range(2):
                     gate_sum(bank[:, i, :], 2 * h + i, 128 * r, 128)
                 live["gate_r%d_%d" % (r, h)] = bank
 
-        def sigm_rows_split(r):
-            for h in range(2):
+        def sigm_rows_split(r, hs=(0, 1)):
+            for h in hs:
                 nc.scalar.activation(
                     out=sig[:, 2 * h : 2 * h + 2, 128 * r : 128 * r + 128], in_=live["gate_r%d_%d" % (r, h)][:], func=SIGMOID
                 )
@@ -185,7 +202,7 @@ def tile_updatespeaker_pa_kernel(
             )
 
         def project(r):
-            bank = flips.tile([P, 512], F32, tag="flip", name="out_%d" % r) if r in [2,3,5] else outs.tile([P, 512], F32, tag="out", name="out_%d" % r)
+            bank = flips.tile([P, 512], F32, tag="flip", name="out_%d" % r) if r in [2,3,4,5,6] else acc.tile([P, 512], F32, tag="acc%d" % (2 + r % 2), name="out_%d" % r)
             nc.tensor.matmul_mx(
                 out=bank[:],
                 lhsT=g_codes[:, 128 * r : 128 * r + 128].bitcast(FP8X4),
@@ -207,7 +224,7 @@ def tile_updatespeaker_pa_kernel(
 
         def project_halves(r):
             for h in range(2):
-                bank = (outs if h else flips).tile([P, 256], F32, tag="out" if h else "flip", name="out_%d_%d" % (r, h))
+                bank = (acc if h else flips).tile([P, 256], F32, tag="acc2" if h else "flip", name="out_%d_%d" % (r, h))
                 nc.tensor.matmul_mx(
                     out=bank[:],
                     lhsT=g_codes[:, 128 * r : 128 * r + 128].bitcast(FP8X4),
@@ -244,27 +261,40 @@ def tile_updatespeaker_pa_kernel(
         nc.scalar.activation(out=warm_out[:], in_=warm_in[:], func=SIGMOID)
         for name, r0, n in LOADS:
             load(name, r0, n)
-        ctx.enter_context(tc.manual_schedule())
+        ctx.enter_context(tc.manual_schedule(engines={mybir.EngineType.PE, mybir.EngineType.SP}))
 
 
-        def prep(k):
-            if k + 1 < 13:
-                for u in PAIRS[k + 1]:
-                    permute(u)
+        def flips_of(k):
             for u in PAIRS[k]:
                 flip(u)
+        def draws_of(k):
             for u in PAIRS[k]:
                 draw(u)
+        def quants_of(k):
             for u in PAIRS[k]:
                 quant(u)
-        for k in range(7):
+        def perms_of(k):
+            for u in PAIRS[k]:
+                permute(u)
+        def prep(k):
+            flips_of(k)
+            draws_of(k)
+            quants_of(k)
+
+        for k in range(3):
             prep(k)
-        gate(0, 0)
+        first_pass(0)
+        prep(3)
+        first_pass(1)
+        prep(4)
+        prep(5)
+        prep(6)
+        first_pass(2)
         prep(7)
-        sigm(0, 0)
-        gate(0, 1)
+        first_pass(3)
+        for t in range(4):
+            first_sigm(t)
         prep(8)
-        sigm(0, 1)
         prep(9)
         gate(1, 0)
         prod(0)
@@ -314,7 +344,7 @@ def tile_updatespeaker_pa_kernel(
         store(5, 1)
         project(6)
         quantg(7)
-        evac(6, "V")
+        evac(6, "S")
         store(6, 1)
         project_halves(7)
         evac_halves(7)

from contextlib import ExitStack

import concourse.mybir as mybir
from concourse.masks import make_identity

F32 = mybir.dt.float32
BF16 = mybir.dt.bfloat16
U32 = mybir.dt.uint32
U8 = mybir.dt.uint8
FP8X4 = mybir.dt.float8_e4m3fn_x4
SIGMOID = mybir.ActivationFunctionType.Sigmoid
MULT = mybir.AluOpType.mult
P = 128
FLOPS = 2 * 1024 * 512 * (1024 + 512 + 512 + 512)

PAIRS = [[["Whp",0,0],["Whp",1,0]],[["hs",0,0],["ha",0,0]],[["Vhp",0,0],["Vhp",1,0]],[["x",0,0],["x",0,1]],[["Wx",0,0],["Wx",0,1]],[["Wx",1,0],["Wx",1,1]],[["hs",1,0],["ha",1,0]],[["x",1,0],["x",1,1]],[["Vhh",0,0],["Vhh",1,0]],[["hs",2,0],["ha",2,0]],[["x",2,0],["x",2,1]],[["hs",3,0],["ha",3,0]],[["x",3,0],["x",3,1]]]
LOADS = [["Whp",0,2],["Whp",2,2],["hs",0,2],["ha",0,2],["Vhp",0,2],["Vhp",2,2],["x",0,2],["Wx",0,2],["Wx",2,2],["hs",2,2],["ha",2,2],["x",2,2],["Vhh",0,4],["hs",4,2],["ha",4,2],["x",4,2],["hs",6,2],["ha",6,2],["x",6,2]]
PERMUTED = []
VECTOR_DRAWS = [["hs",0,0],["Vhp",1,0],["Wx",0,0],["Wx",1,1],["x",1,0],["Vhh",1,0],["x",2,0],["ha",3,0]]


def tile_updatespeaker_pa_kernel(
    tc, encoder_hidden, spk_vectors, adr_vectors, WA_xp, WA_hp, VA_hp, VA_hh, out
):
    nc = tc.nc
    with ExitStack() as ctx:
        keep = ctx.enter_context(tc.tile_pool(name="keep", bufs=1))
        flips = ctx.enter_context(tc.psum_pool(name="flips", bufs=4))
        acc = ctx.enter_context(tc.psum_pool(name="acc", bufs=1))

        ident = keep.tile([P, P], F32, name="ident")
        warm_in = keep.tile([P, 1], F32, name="warm_in")
        warm_out = keep.tile([P, 1], F32, name="warm_out")

        raw = {}
        for name, rows, width in (
            ("Whp", 4, 512), ("Vhp", 4, 512), ("Vhh", 4, 512), ("Wx", 4, 1024), ("hs", 8, 512), ("ha", 8, 512), ("x", 8, 1024)
        ):
            raw[name] = keep.tile([P, rows, width], BF16, name=name + "_raw")

        hbm = {
            "Whp": WA_hp.rearrange("(p t) k -> p t k", t=4),
            "Vhp": VA_hp.rearrange("(p t) k -> p t k", t=4),
            "Wx": WA_xp.rearrange("(p t) k -> p t k", t=4),
            "Vhh": VA_hh.rearrange("(j p) k -> p j k", p=P),
            "hs": spk_vectors.rearrange("(p r) k -> p r k", r=8),
            "ha": adr_vectors.rearrange("(p r) k -> p r k", r=8),
            "x": encoder_hidden.rearrange("(p r) k -> p r k", r=8),
        }

        grp = {}
        codes = {}
        scl = {}
        for name, width in (
            ("Whp", 512), ("Vhp", 512), ("Wxk0", 512), ("Wxk1", 512), ("Vhh", 512),
            ("hs", 1024), ("ha", 1024), ("xk0", 1024), ("xk1", 1024),
        ):
            grp[name] = keep.tile([P, width, 2], F32, name="grp_" + name, align_bytes=64)
            codes[name] = keep.tile([P, width], U32, name="codes_" + name, align_bytes=64)
            scl[name] = keep.tile([P, width], U8, name="scl_" + name, align_bytes=64)
        g_grp = keep.tile([P, 1024, 4], BF16, name="g_grp", align_bytes=64)
        g_codes = keep.tile([P, 1024], U32, name="g_codes", align_bytes=64)
        g_scl = keep.tile([P, 1024], U8, name="g_scl", align_bytes=64)
        sig = keep.tile([P, 4, 1024], F32, name="sig")
        o_sb = keep.tile([P, 8, 512], F32, name="o_sb")

        def load(name, r0, n):
            nc.sync.dma_start(out=raw[name][:, r0 : r0 + n, :], in_=hbm[name][:, r0 : r0 + n, :])

        def parts(unit):
            name, i, g = unit
            dst = name + "k%d" % g if name in ("x", "Wx") else name
            return name, 2 * i, 256 * g, dst, 256 * i

        live = {}
        count = [0]
        perm = {}

        def flip(unit):
            name, row, w0, dst, c0 = parts(unit)
            label = "%s_%d_%d" % (name, row, w0)
            words = raw[name][:].bitcast(F32)
            bank = flips.tile([P, 2, 256], F32, tag="flip", name="flip_" + label)
            if unit in PERMUTED:
                pm = perm[tuple(unit)]
            for i in range(2):
                for half in range(2):
                    if unit in PERMUTED:
                        src = pm[:, i, half, :]
                    else:
                        src = words[:, row + i, w0 + half : w0 + 256 : 2]
                    nc.tensor.transpose(bank[:, half, 128 * i : 128 * i + 128], src, ident[:])
            live[label] = bank

        def permute(unit):
            if unit not in PERMUTED:
                return
            name, row, w0, dst, c0 = parts(unit)
            label = "%s_%d_%d" % (name, row, w0)
            words = raw[name][:].bitcast(F32)
            pm = keep.tile([P, 2, 2, 128], F32, name="perm_" + label)
            perm[tuple(unit)] = pm
            nc.vector.tensor_copy(
                out=pm[:], in_=words[:, row : row + 2, w0 : w0 + 256].rearrange("p r (m u) -> p r u m", u=2)
            )

        def draw(unit):
            name, row, w0, dst, c0 = parts(unit)
            label = "%s_%d_%d" % (name, row, w0)
            src = live[label][:].rearrange("p u c -> p c u")
            if unit in VECTOR_DRAWS:
                nc.vector.tensor_copy(out=grp[dst][:, c0 : c0 + 256, :], in_=src)
            else:
                nc.scalar.copy(out=grp[dst][:, c0 : c0 + 256, :], in_=src)

        def quant(unit):
            name, row, w0, dst, c0 = parts(unit)
            nc.vector.quantize_mx(
                out=codes[dst][:, c0 : c0 + 256].bitcast(FP8X4),
                scales=scl[dst][:, c0 : c0 + 256],
                in_=grp[dst][:].bitcast(BF16)[:, c0 : c0 + 256, :].rearrange("p c t -> p (c t)"),
            )

        SUMS = (("Whp", "hs"), ("Vhp", "ha"), ("Wxk0", "xk0"), ("Wxk1", "xk1"))

        def gate_sum(dst, t, c0, n):
            for s, (w, a) in enumerate(SUMS):
                nc.tensor.matmul_mx(
                    out=dst,
                    lhsT=codes[w][:, 128 * t : 128 * t + 128].bitcast(FP8X4),
                    lhsT_scale=scl[w][:, 128 * t : 128 * t + 128],
                    rhs=codes[a][:, c0 : c0 + n].bitcast(FP8X4),
                    rhs_scale=scl[a][:, c0 : c0 + n],
                    start=s == 0,
                    stop=s == 3,
                )

        def first_pass(s):
            w, a = SUMS[s]
            for t in range(4):
                if s == 0:
                    live["first_%d" % t] = acc.tile([P, 256], F32, tag="acc%d" % t, name="first_%d" % t)
                nc.tensor.matmul_mx(
                    out=live["first_%d" % t][:],
                    lhsT=codes[w][:, 128 * t : 128 * t + 128].bitcast(FP8X4),
                    lhsT_scale=scl[w][:, 128 * t : 128 * t + 128],
                    rhs=codes[a][:, 0:256].bitcast(FP8X4),
                    rhs_scale=scl[a][:, 0:256],
                    start=s == 0,
                    stop=s == 3,
                )

        def first_sigm(t):
            nc.scalar.activation(out=sig[:, t, 0:256], in_=live["first_%d" % t][:], func=SIGMOID)

        def gate(j, h):
            bank = acc.tile([P, 2, 256], F32, tag="acc%d" % h, name="gate_%d_%d" % (j, h))
            for i in range(2):
                gate_sum(bank[:, i, :], 2 * h + i, 256 * j, 256)
            live["gate_%d_%d" % (j, h)] = bank

        def sigm(j, h):
            nc.scalar.activation(
                out=sig[:, 2 * h : 2 * h + 2, 256 * j : 256 * j + 256], in_=live["gate_%d_%d" % (j, h)][:], func=SIGMOID
            )

        def gate_rows(r):
            bank = acc.tile([P, 4, 128], F32, tag="acc%d" % (r % 2), name="gate_r%d" % r)
            for t in range(4):
                gate_sum(bank[:, t, :], t, 128 * r, 128)
            live["gate_r%d" % r] = bank

        def gate_rows_split(r, hs=(0, 1)):
            for h in hs:
                bank = flips.tile([P, 2, 128], F32, tag="flip", name="gate_r%d_%d" % (r, h))
                for i in range(2):
                    gate_sum(bank[:, i, :], 2 * h + i, 128 * r, 128)
                live["gate_r%d_%d" % (r, h)] = bank

        def sigm_rows_split(r, hs=(0, 1)):
            for h in hs:
                nc.scalar.activation(
                    out=sig[:, 2 * h : 2 * h + 2, 128 * r : 128 * r + 128], in_=live["gate_r%d_%d" % (r, h)][:], func=SIGMOID
                )

        def sigm_rows(r):
            nc.scalar.activation(out=sig[:, :, 128 * r : 128 * r + 128], in_=live["gate_r%d" % r][:], func=SIGMOID)

        def prod(r):
            nc.vector.tensor_tensor(
                out=g_grp[:, 128 * r : 128 * r + 128, :],
                in0=sig[:, :, 128 * r : 128 * r + 128].rearrange("p t b -> p b t"),
                in1=grp["ha"][:].bitcast(BF16)[:, 128 * r : 128 * r + 128, :],
                op=MULT,
            )

        def quantg(r):
            nc.vector.quantize_mx(
                out=g_codes[:, 128 * r : 128 * r + 128].bitcast(FP8X4),
                scales=g_scl[:, 128 * r : 128 * r + 128],
                in_=g_grp[:, 128 * r : 128 * r + 128, :].rearrange("p c t -> p (c t)"),
            )

        def project(r):
            bank = flips.tile([P, 512], F32, tag="flip", name="out_%d" % r) if r in [2,3,4,5,6] else acc.tile([P, 512], F32, tag="acc%d" % (2 + r % 2), name="out_%d" % r)
            nc.tensor.matmul_mx(
                out=bank[:],
                lhsT=g_codes[:, 128 * r : 128 * r + 128].bitcast(FP8X4),
                lhsT_scale=g_scl[:, 128 * r : 128 * r + 128],
                rhs=codes["Vhh"][:].bitcast(FP8X4),
                rhs_scale=scl["Vhh"][:],
                start=True,
                stop=True,
            )
            live["out_%d" % r] = bank

        def evac(r, eng):
            src = live["out_%d" % r][:]
            dst = o_sb[:, r, :]
            if eng == "V":
                nc.vector.tensor_copy(out=dst, in_=src)
            else:
                nc.scalar.copy(out=dst, in_=src)

        def project_halves(r):
            for h in range(2):
                bank = (acc if h else flips).tile([P, 256], F32, tag="acc2" if h else "flip", name="out_%d_%d" % (r, h))
                nc.tensor.matmul_mx(
                    out=bank[:],
                    lhsT=g_codes[:, 128 * r : 128 * r + 128].bitcast(FP8X4),
                    lhsT_scale=g_scl[:, 128 * r : 128 * r + 128],
                    rhs=codes["Vhh"][:, 256 * h : 256 * h + 256].bitcast(FP8X4),
                    rhs_scale=scl["Vhh"][:, 256 * h : 256 * h + 256],
                    start=True,
                    stop=True,
                )
                live["out_%d_%d" % (r, h)] = bank

        def evac_halves(r):
            for h in range(2):
                src = live["out_%d_%d" % (r, h)][:]
                dst = o_sb[:, r, 256 * h : 256 * h + 256]
                if h:
                    nc.scalar.copy(out=dst, in_=src)
                else:
                    nc.vector.tensor_copy(out=dst, in_=src)

        def store_half(r, h):
            nc.sync.dma_start(
                out=out.rearrange("(p r) o -> p r o", r=8)[:, r, 256 * h : 256 * h + 256],
                in_=o_sb[:, r, 256 * h : 256 * h + 256],
            )

        def store(r0, n):
            nc.sync.dma_start(
                out=out.rearrange("(p r) o -> p r o", r=8)[:, r0 : r0 + n, :], in_=o_sb[:, r0 : r0 + n, :]
            )

        nc.vector.memset(warm_in[:], 0.0)
        make_identity(nc, ident[:])
        nc.scalar.activation(out=warm_out[:], in_=warm_in[:], func=SIGMOID)
        for name, r0, n in LOADS:
            load(name, r0, n)
        ctx.enter_context(tc.manual_schedule(engines={mybir.EngineType.PE, mybir.EngineType.SP}))


        def flips_of(k):
            for u in PAIRS[k]:
                flip(u)
        def draws_of(k):
            for u in PAIRS[k]:
                draw(u)
        def quants_of(k):
            for u in PAIRS[k]:
                quant(u)
        def perms_of(k):
            for u in PAIRS[k]:
                permute(u)
        def prep(k):
            flips_of(k)
            draws_of(k)
            quants_of(k)

        for k in range(3):
            prep(k)
        first_pass(0)
        prep(3)
        first_pass(1)
        prep(4)
        prep(5)
        prep(6)
        first_pass(2)
        prep(7)
        first_pass(3)
        for t in range(4):
            first_sigm(t)
        prep(8)
        prep(9)
        gate(1, 0)
        prod(0)
        sigm(1, 0)
        prod(1)
        quantg(0)
        prep(10)
        quantg(1)
        gate(1, 1)
        sigm(1, 1)
        prep(11)
        prod(2)
        project(0)
        prep(12)
        prod(3)
        quantg(2)
        gate(2, 0)
        quantg(3)
        evac(0, "S")
        sigm(2, 0)
        project(1)
        gate(2, 1)
        evac(1, "V")
        sigm(2, 1)
        store(0, 2)
        project(2)
        project(3)
        gate_rows(6)
        prod(4)
        evac(2, "S")
        prod(5)
        quantg(4)
        evac(3, "S")
        sigm_rows(6)
        quantg(5)
        store(2, 2)
        gate_rows_split(7)
        prod(6)
        sigm_rows_split(7)
        project(4)
        quantg(6)
        evac(4, "S")
        store(4, 1)
        project(5)
        prod(7)
        evac(5, "S")
        store(5, 1)
        project(6)
        quantg(7)
        evac(6, "S")
        store(6, 1)
        project_halves(7)
        evac_halves(7)
        store_half(7, 0)
        store_half(7, 1)
